import numpy as np
import ml_dtypes


def mxq(x, axis, fmt="e4m3"):
    dtype, down = {"e4m3": (ml_dtypes.float8_e4m3fn, 7), "e5m2": (ml_dtypes.float8_e5m2, 14)}[fmt]
    v = np.moveaxis(np.asarray(x, np.float32).astype(ml_dtypes.bfloat16).astype(np.float64), axis, -1)
    blocks = v.reshape(v.shape[:-1] + (-1, 32))
    amax = np.abs(blocks).max(-1, keepdims=True)
    byte = np.maximum(np.where(amax > 0, np.frexp(amax)[1] - 1 + 127, 0) - down, 1)
    scale = np.exp2(byte - 127.0)
    codes = (blocks / scale).astype(np.float32).astype(dtype).astype(np.float64)
    return np.moveaxis((codes * scale).reshape(v.shape), -1, axis)


WIDE = False


def mx_kscale(k):
    if not WIDE:
        return np.ones(k)
    levels = np.array([10, -10, 5, -5, 0])
    if k % 512:
        return np.exp2(np.random.permutation(np.resize(levels, k // 32))).repeat(32)
    a = np.empty((k // 512, 16))
    for p in range(k // 512):
        a[p, :8] = np.random.permutation(np.resize(levels, 8))
        for g in range(8):
            far = levels[np.abs(levels - a[p, g]) >= 10]
            a[p, g + 8] = far[np.random.randint(len(far))]
    return np.exp2(a.ravel()).repeat(32)


BF16 = ml_dtypes.bfloat16


def bf(x):
    return np.asarray(x, np.float32).astype(BF16)


def f64(x):
    return np.asarray(x).astype(np.float64)


B, A, C, P = 64, 7, 1024, 1024
N = A * A + 1


def scramble(y):
    return y.transpose(0, 2, 1).reshape(B, N, C)


def unscramble(z):
    return z.reshape(B, C, N).transpose(0, 2, 1)


def setup_inputs():
    s = mx_kscale(C)
    z = np.random.standard_normal((B, N, C)) * 1.6 / np.sqrt(N) * s
    return {"y_attn": bf(np.ascontiguousarray(unscramble(z))),
            "w_proj": bf(np.random.standard_normal((P, C)) * 2.0 / np.sqrt(C) / s),
            "b_proj": bf(np.random.standard_normal(P) * 0.1)}


def reference(y_attn, w_proj, b_proj):
    z = scramble(f64(y_attn))
    return (mxq(z, 2, "e4m3") @ mxq(f64(w_proj), 1, "e4m3").T) + f64(b_proj)

@@ -1,0 +1,199 @@
+import concourse.mybir as mybir
+from concourse.masks import make_identity
+
+F32 = mybir.dt.float32
+BF16 = mybir.dt.bfloat16
+U32 = mybir.dt.uint32
+U8 = mybir.dt.uint8
+FP8X4 = mybir.dt.float8_e4m3fn_x4
+ADD = mybir.AluOpType.add
+MULT = mybir.AluOpType.mult
+
+P = 128
+IMAGES = 64
+TOKENS = 50
+CHANNELS = 1024
+FEATURES = 1024
+K = 1024
+HALVES = 2
+HALF_CHANNELS = CHANNELS // HALVES
+ROWS = TOKENS // HALVES
+PACK = 4
+K_PASS = P * PACK
+PASSES = K // K_PASS
+WORDS = K // 2
+PLANES = WORDS // P
+N_TILE = 512
+N_TILES = FEATURES // N_TILE
+W_TILES = FEATURES // P
+GROUP = 2
+LEAD = 1
+AHEAD = 2
+RUN = 4
+SLAB = 16
+CHUNKS = (128, 128, 256)
+VECTOR_FIRST = 32
+GPSIMD_SHARE = 8
+RESULT_ROWS = 14
+
+FLOPS = 2 * IMAGES * TOKENS * K * FEATURES
+
+
+def transpose_row_tile(nc, bank, rows_bf16, identity):
+    words = rows_bf16.bitcast(F32)
+    for v in range(PLANES):
+        g, u = divmod(v, 2)
+        nc.tensor.transpose(bank[:, v, :], words[:, g * 2 * P + u : (g + 1) * 2 * P : 2], identity)
+
+
+def planes_side_by_side(bank):
+    return bank.rearrange("p (g u) r -> p g r u", g=PASSES)
+
+
+def channels_through(rows):
+    return min(HALF_CHANNELS, -(-rows * K // (TOKENS * SLAB)) * SLAB)
+
+
+def tile_attention_pa_kernel(tc, y_attn, w_proj, b_proj, out):
+    nc = tc.nc
+    out_rows = out.rearrange("b (a i) f -> (b a) i f", a=HALVES)
+    w_tiles = w_proj.rearrange("(t p) j -> p t j", p=P)
+    half_w = W_TILES // N_TILES
+
+    with tc.tile_pool(name="keep", bufs=1) as keep, tc.tile_pool(name="zq", bufs=LEAD + 2) as zq, tc.tile_pool(
+        name="results", bufs=RESULT_ROWS
+    ) as results, tc.psum_pool(name="planes", bufs=4) as planes, tc.psum_pool(
+        name="sums", bufs=4
+    ) as sums, tc.manual_schedule():
+        bias_rows = keep.tile([P, FEATURES], BF16)
+        nc.vector.memset(bias_rows[:], 0.0)
+        ones = keep.tile([P, P], BF16)
+        nc.vector.memset(ones[:], 1.0)
+        identity = keep.tile([P, P], F32)
+        make_identity(nc, identity[:])
+
+        w_raw = keep.tile([P, W_TILES, K], BF16)
+        for h in range(N_TILES):
+            nc.sync.dma_start(
+                out=w_raw[:, h * half_w : (h + 1) * half_w, :], in_=w_tiles[:, h * half_w : (h + 1) * half_w, :]
+            )
+        nc.sync.dma_start(out=bias_rows[0:1, :], in_=b_proj.rearrange("(o f) -> o f", o=1))
+        y_chunks = []
+        first_channel = 0
+        for c, width in enumerate(CHUNKS):
+            y_chunk = keep.tile([P, TOKENS, width], BF16, name="y_chunk%d" % c)
+            for a in range(HALVES):
+                lo = a * HALF_CHANNELS + first_channel
+                nc.sync.dma_start(out=y_chunk[a:P:HALVES, :, :], in_=y_attn[:, :, lo : lo + width])
+            y_chunks.append((y_chunk, first_channel, width))
+            first_channel += width
+
+        w_grouped = keep.tile([P, PASSES, FEATURES * PACK], BF16, align_bytes=64)
+        w_codes = keep.tile([P, PASSES, FEATURES], U32, align_bytes=64)
+        w_scales = keep.tile([P, PASSES, FEATURES], U8, align_bytes=64)
+        for t in range(W_TILES):
+            bank = planes.tile([P, PLANES, P], F32, tag="bank")
+            transpose_row_tile(nc, bank, w_raw[:, t, :], identity[:])
+            target = w_grouped[:, :, t * P * PACK : (t + 1) * P * PACK].bitcast(F32)
+            target = target.rearrange("p g (r u) -> p g r u", u=2)
+            if t % 2 == 0:
+                nc.vector.tensor_copy(out=target, in_=planes_side_by_side(bank))
+            else:
+                nc.scalar.copy(out=target, in_=planes_side_by_side(bank))
+            if (t + 1) % half_w == 0:
+                h = t // half_w
+                for g in range(PASSES):
+                    nc.vector.quantize_mx(
+                        out=w_codes[:, g, h * N_TILE : (h + 1) * N_TILE].bitcast(FP8X4),
+                        scales=w_scales[:, g, h * N_TILE : (h + 1) * N_TILE],
+                        in_=w_grouped[:, g, h * N_TILE * PACK : (h + 1) * N_TILE * PACK],
+                    )
+
+        bias = keep.tile([P, FEATURES], F32)
+        for h in range(N_TILES):
+            cols = slice(h * N_TILE, (h + 1) * N_TILE)
+            spread = sums.tile([P, N_TILE], F32, tag="acc")
+            nc.tensor.matmul(out=spread[:], lhsT=ones[:], rhs=bias_rows[:, cols], start=True, stop=True)
+            nc.vector.tensor_copy(out=bias[:, cols], in_=spread[:])
+
+        z_flat = keep.tile([P, ROWS * K], BF16, align_bytes=64)
+        groups = [(first, min(GROUP, ROWS - first)) for first in range(0, ROWS, GROUP)]
+        quantised = {}
+
+        def interleave_views(lo, hi):
+            y_chunk, first_channel, width = [c for c in y_chunks if c[1] <= lo < c[1] + c[2]][0]
+            assert hi <= first_channel + width
+            dst = z_flat[:, TOKENS * lo : TOKENS * hi].rearrange("p (c i n) -> p c n i", i=RUN, n=TOKENS)
+            src = y_chunk[:, :, lo - first_channel : hi - first_channel].rearrange("p n (c i) -> p c n i", i=RUN)
+            return dst, src
+
+        def interleave(index, before_the_sums):
+            lo = channels_through(groups[index][0])
+            hi = channels_through(groups[index][0] + groups[index][1])
+            if before_the_sums:
+                vector_end = min(hi, lo + VECTOR_FIRST)
+                dst, src = interleave_views(lo, vector_end)
+                nc.vector.tensor_copy(out=dst, in_=src)
+                if vector_end < hi:
+                    dst, src = interleave_views(vector_end, hi)
+                    nc.scalar.copy(out=dst, in_=src)
+            else:
+                scalar_end = lo + (hi - lo) // 2
+                dst, src = interleave_views(lo, scalar_end)
+                nc.scalar.copy(out=dst, in_=src)
+                gpsimd_end = min(hi, scalar_end + GPSIMD_SHARE)
+                if scalar_end < gpsimd_end:
+                    dst, src = interleave_views(scalar_end, gpsimd_end)
+                    nc.gpsimd.tensor_scalar(out=dst, in0=src, scalar1=1.0, scalar2=0.0, op0=MULT, op1=ADD)
+                if gpsimd_end < hi:
+                    dst, src = interleave_views(gpsimd_end, hi)
+                    nc.vector.tensor_copy(out=dst, in_=src)
+
+        def prepare(index):
+            first, count = groups[index]
+            z_grouped = zq.tile([P, GROUP, PASSES * P * PACK], BF16, align_bytes=64)
+            z_codes = zq.tile([P, GROUP, PASSES * P], U32, align_bytes=64)
+            z_scales = zq.tile([P, GROUP, PASSES * P], U8, align_bytes=64)
+            for r in range(count):
+                bank = planes.tile([P, PLANES, P], F32, tag="bank")
+                transpose_row_tile(nc, bank, z_flat[:, (first + r) * K : (first + r + 1) * K], identity[:])
+                target = z_grouped[:, r, :].bitcast(F32).rearrange("p (g r u) -> p g r u", g=PASSES, u=2)
+                nc.scalar.copy(out=target, in_=planes_side_by_side(bank))
+            for r in range(count):
+                nc.vector.quantize_mx(
+                    out=z_codes[:, r, :].bitcast(FP8X4), scales=z_scales[:, r, :], in_=z_grouped[:, r, :]
+                )
+            quantised[index] = (z_codes, z_scales)
+
+        def multiply(index):
+            first, count = groups[index]
+            z_codes, z_scales = quantised[index]
+            for r in range(count):
+                result = results.tile([P, FEATURES], F32)
+                for h in range(N_TILES):
+                    cols = slice(h * N_TILE, (h + 1) * N_TILE)
+                    acc = sums.tile([P, N_TILE], F32, tag="acc")
+                    for g in range(PASSES):
+                        nc.tensor.matmul_mx(
+                            out=acc[:],
+                            lhsT=z_codes[:, r, g * P : (g + 1) * P].bitcast(FP8X4),
+                            lhsT_scale=z_scales[:, r, g * P : (g + 1) * P],
+                            rhs=w_codes[:, g, cols].bitcast(FP8X4),
+                            rhs_scale=w_scales[:, g, cols],
+                            start=(g == 0),
+                            stop=(g == PASSES - 1),
+                        )
+                    if r == 1 and h == 0:
+                        nc.scalar.copy(out=result[:, cols], in_=acc[:])
+                        nc.gpsimd.tensor_tensor(out=result[:, cols], in0=result[:, cols], in1=bias[:, cols], op=ADD)
+                    else:
+                        nc.vector.tensor_tensor(out=result[:, cols], in0=acc[:], in1=bias[:, cols], op=ADD)
+                nc.sync.dma_start(out=out_rows[:, first + r, :], in_=result[:])
+
+        for step in range(-(LEAD + AHEAD), len(groups)):
+            if 0 <= step + LEAD < len(groups):
+                prepare(step + LEAD)
+            if step >= 0:
+                multiply(step)
+            if step + LEAD + AHEAD < len(groups):
+                interleave(step + LEAD + AHEAD, step < 0)

@@ -18,36 +18,23 @@ K = 1024
 HALVES = 2
 HALF_CHANNELS = CHANNELS // HALVES
 ROWS = TOKENS // HALVES
+PARITIES = 2
+PAIRS = TOKENS // PARITIES
 PACK = 4
 K_PASS = P * PACK
 PASSES = K // K_PASS
-WORDS = K // 2
-PLANES = WORDS // P
+BANK_PLANES = PASSES * 2
 N_TILE = 512
 N_TILES = FEATURES // N_TILE
 W_TILES = FEATURES // P
+HALF_W = W_TILES // N_TILES
 GROUP = 2
-LEAD = 1
-AHEAD = 2
 RUN = 4
 SLAB = 16
-CHUNKS = (128, 128, 256)
-VECTOR_FIRST = 32
-GPSIMD_SHARE = 8
-RESULT_ROWS = 14
+CHUNK = 256
+RESULT_ROWS = 10
 
 FLOPS = 2 * IMAGES * TOKENS * K * FEATURES
-
-
-def transpose_row_tile(nc, bank, rows_bf16, identity):
-    words = rows_bf16.bitcast(F32)
-    for v in range(PLANES):
-        g, u = divmod(v, 2)
-        nc.tensor.transpose(bank[:, v, :], words[:, g * 2 * P + u : (g + 1) * 2 * P : 2], identity)
-
-
-def planes_side_by_side(bank):
-    return bank.rearrange("p (g u) r -> p g r u", g=PASSES)
 
 
 def channels_through(rows):
@@ -58,9 +45,9 @@ def tile_attention_pa_kernel(tc, y_attn, w_proj, b_proj, out):
     nc = tc.nc
     out_rows = out.rearrange("b (a i) f -> (b a) i f", a=HALVES)
     w_tiles = w_proj.rearrange("(t p) j -> p t j", p=P)
-    half_w = W_TILES // N_TILES
+    y_tokens = y_attn.rearrange("b (m u) c -> b u m c", u=PARITIES)
 
-    with tc.tile_pool(name="keep", bufs=1) as keep, tc.tile_pool(name="zq", bufs=LEAD + 2) as zq, tc.tile_pool(
+    with tc.tile_pool(name="keep", bufs=1) as keep, tc.tile_pool(name="zq", bufs=4) as zq, tc.tile_pool(
         name="results", bufs=RESULT_ROWS
     ) as results, tc.psum_pool(name="planes", bufs=4) as planes, tc.psum_pool(
         name="sums", bufs=4
@@ -73,104 +60,114 @@ def tile_attention_pa_kernel(tc, y_attn, w_proj, b_proj, out):
         make_identity(nc, identity[:])
 
         w_raw = keep.tile([P, W_TILES, K], BF16)
-        for h in range(N_TILES):
-            nc.sync.dma_start(
-                out=w_raw[:, h * half_w : (h + 1) * half_w, :], in_=w_tiles[:, h * half_w : (h + 1) * half_w, :]
-            )
-        nc.sync.dma_start(out=bias_rows[0:1, :], in_=b_proj.rearrange("(o f) -> o f", o=1))
         y_chunks = []
-        first_channel = 0
-        for c, width in enumerate(CHUNKS):
-            y_chunk = keep.tile([P, TOKENS, width], BF16, name="y_chunk%d" % c)
-            for a in range(HALVES):
-                lo = a * HALF_CHANNELS + first_channel
-                nc.sync.dma_start(out=y_chunk[a:P:HALVES, :, :], in_=y_attn[:, :, lo : lo + width])
-            y_chunks.append((y_chunk, first_channel, width))
-            first_channel += width
+
+        def load_w(first, count):
+            nc.sync.dma_start(out=w_raw[:, first : first + count, :], in_=w_tiles[:, first : first + count, :])
+
+        def load_y(c):
+            y_chunk = keep.tile([P, PARITIES, PAIRS, CHUNK], BF16, name="y_chunk%d" % c)
+            for u in range(PARITIES):
+                for a in range(HALVES):
+                    lo = a * HALF_CHANNELS + c * CHUNK
+                    nc.sync.dma_start(out=y_chunk[a:P:HALVES, u, :, :], in_=y_tokens[:, u, :, lo : lo + CHUNK])
+            y_chunks.append(y_chunk)
+
+        load_w(0, HALF_W)
+        nc.sync.dma_start(out=bias_rows[0:1, :], in_=b_proj.rearrange("(o f) -> o f", o=1))
+        load_y(0)
+        load_w(HALF_W, HALF_W // 2)
+        load_w(HALF_W + HALF_W // 2, HALF_W // 2)
+        load_y(1)
 
         w_grouped = keep.tile([P, PASSES, FEATURES * PACK], BF16, align_bytes=64)
         w_codes = keep.tile([P, PASSES, FEATURES], U32, align_bytes=64)
         w_scales = keep.tile([P, PASSES, FEATURES], U8, align_bytes=64)
-        for t in range(W_TILES):
-            bank = planes.tile([P, PLANES, P], F32, tag="bank")
-            transpose_row_tile(nc, bank, w_raw[:, t, :], identity[:])
-            target = w_grouped[:, :, t * P * PACK : (t + 1) * P * PACK].bitcast(F32)
-            target = target.rearrange("p g (r u) -> p g r u", u=2)
-            if t % 2 == 0:
-                nc.vector.tensor_copy(out=target, in_=planes_side_by_side(bank))
-            else:
-                nc.scalar.copy(out=target, in_=planes_side_by_side(bank))
-            if (t + 1) % half_w == 0:
-                h = t // half_w
-                for g in range(PASSES):
-                    nc.vector.quantize_mx(
-                        out=w_codes[:, g, h * N_TILE : (h + 1) * N_TILE].bitcast(FP8X4),
-                        scales=w_scales[:, g, h * N_TILE : (h + 1) * N_TILE],
-                        in_=w_grouped[:, g, h * N_TILE * PACK : (h + 1) * N_TILE * PACK],
-                    )
 
-        bias = keep.tile([P, FEATURES], F32)
-        for h in range(N_TILES):
-            cols = slice(h * N_TILE, (h + 1) * N_TILE)
-            spread = sums.tile([P, N_TILE], F32, tag="acc")
-            nc.tensor.matmul(out=spread[:], lhsT=ones[:], rhs=bias_rows[:, cols], start=True, stop=True)
-            nc.vector.tensor_copy(out=bias[:, cols], in_=spread[:])
+        def prepare_w(t):
+            bank = planes.tile([P, BANK_PLANES, P], F32, tag="bank")
+            words = w_raw[:, t, :].bitcast(F32)
+            for v in range(BANK_PLANES):
+                g, x = divmod(v, 2)
+                nc.tensor.transpose(bank[:, v, :], words[:, g * 2 * P + x : (g + 1) * 2 * P : 2], identity[:])
+            target = w_grouped[:, :, t * P * PACK : (t + 1) * P * PACK].rearrange("p g (r y x) -> p g r y x", y=2, x=2)
+            source = bank[:].rearrange("p v r -> p (v r)").bitcast(BF16)
+            source = source.rearrange("p (g x r y) -> p g r y x", g=PASSES, x=2, y=2)
+            for g in range(PASSES):
+                if t % 2 == 0:
+                    nc.vector.tensor_copy(out=target[:, g], in_=source[:, g])
+                else:
+                    nc.scalar.copy(out=target[:, g], in_=source[:, g])
 
-        z_flat = keep.tile([P, ROWS * K], BF16, align_bytes=64)
+        def quantise_w(first, count):
+            for g in range(PASSES):
+                nc.vector.quantize_mx(
+                    out=w_codes[:, g, first * P : (first + count) * P].bitcast(FP8X4),
+                    scales=w_scales[:, g, first * P : (first + count) * P],
+                    in_=w_grouped[:, g, first * P * PACK : (first + count) * P * PACK],
+                )
+
+        z_planes = keep.tile([P, PARITIES, ROWS * K // PARITIES], BF16, align_bytes=64)
         groups = [(first, min(GROUP, ROWS - first)) for first in range(0, ROWS, GROUP)]
+        reach = [0] + [channels_through(first + count) for first, count in groups]
         quantised = {}
+        row_results = {}
 
-        def interleave_views(lo, hi):
-            y_chunk, first_channel, width = [c for c in y_chunks if c[1] <= lo < c[1] + c[2]][0]
-            assert hi <= first_channel + width
-            dst = z_flat[:, TOKENS * lo : TOKENS * hi].rearrange("p (c i n) -> p c n i", i=RUN, n=TOKENS)
-            src = y_chunk[:, :, lo - first_channel : hi - first_channel].rearrange("p n (c i) -> p c n i", i=RUN)
-            return dst, src
-
-        def interleave(index, before_the_sums):
-            lo = channels_through(groups[index][0])
-            hi = channels_through(groups[index][0] + groups[index][1])
-            if before_the_sums:
-                vector_end = min(hi, lo + VECTOR_FIRST)
-                dst, src = interleave_views(lo, vector_end)
+        def interleave(engine, u, lo, hi):
+            if lo >= hi:
+                return
+            c = lo // CHUNK
+            if hi > (c + 1) * CHUNK:
+                interleave(engine, u, lo, (c + 1) * CHUNK)
+                interleave(engine, u, (c + 1) * CHUNK, hi)
+                return
+            dst = z_planes[:, u, PAIRS * lo : PAIRS * hi].rearrange("p (c i m) -> p c m i", i=RUN, m=PAIRS)
+            src = y_chunks[c][:, u, :, lo - c * CHUNK : hi - c * CHUNK].rearrange("p m (c i) -> p c m i", i=RUN)
+            if engine == "vector":
                 nc.vector.tensor_copy(out=dst, in_=src)
-                if vector_end < hi:
-                    dst, src = interleave_views(vector_end, hi)
-                    nc.scalar.copy(out=dst, in_=src)
-            else:
-                scalar_end = lo + (hi - lo) // 2
-                dst, src = interleave_views(lo, scalar_end)
+            elif engine == "scalar":
                 nc.scalar.copy(out=dst, in_=src)
-                gpsimd_end = min(hi, scalar_end + GPSIMD_SHARE)
-                if scalar_end < gpsimd_end:
-                    dst, src = interleave_views(scalar_end, gpsimd_end)
-                    nc.gpsimd.tensor_scalar(out=dst, in0=src, scalar1=1.0, scalar2=0.0, op0=MULT, op1=ADD)
-                if gpsimd_end < hi:
-                    dst, src = interleave_views(gpsimd_end, hi)
-                    nc.vector.tensor_copy(out=dst, in_=src)
+            else:
+                nc.gpsimd.tensor_scalar(out=dst, in0=src, scalar1=1.0, scalar2=0.0, op0=MULT, op1=ADD)
 
-        def prepare(index):
+        def transpose_rows(index, engines):
             first, count = groups[index]
             z_grouped = zq.tile([P, GROUP, PASSES * P * PACK], BF16, align_bytes=64)
+            for r in range(count):
+                bank = planes.tile([P, BANK_PLANES, P], F32, tag="bank")
+                for v in range(BANK_PLANES):
+                    g, u = divmod(v, 2)
+                    start = ((first + r) * K + g * K_PASS) // PARITIES
+                    words = z_planes[:, u, start : start + K_PASS // PARITIES].bitcast(F32)
+                    nc.tensor.transpose(bank[:, v, :], words, identity[:])
+                target = z_grouped[:, r, :].bitcast(F32).rearrange("p (g r u) -> p g r u", g=PASSES, u=2)
+                source = bank[:].rearrange("p (g u) r -> p g r u", g=PASSES)
+                if engines[r] == "vector":
+                    nc.vector.tensor_copy(out=target, in_=source)
+                else:
+                    nc.scalar.copy(out=target, in_=source)
+            quantised[index] = [z_grouped]
+
+        def quantise(index):
+            first, count = groups[index]
+            z_grouped = quantised[index][0]
             z_codes = zq.tile([P, GROUP, PASSES * P], U32, align_bytes=64)
             z_scales = zq.tile([P, GROUP, PASSES * P], U8, align_bytes=64)
-            for r in range(count):
-                bank = planes.tile([P, PLANES, P], F32, tag="bank")
-                transpose_row_tile(nc, bank, z_flat[:, (first + r) * K : (first + r + 1) * K], identity[:])
-                target = z_grouped[:, r, :].bitcast(F32).rearrange("p (g r u) -> p g r u", g=PASSES, u=2)
-                nc.scalar.copy(out=target, in_=planes_side_by_side(bank))
             for r in range(count):
                 nc.vector.quantize_mx(
                     out=z_codes[:, r, :].bitcast(FP8X4), scales=z_scales[:, r, :], in_=z_grouped[:, r, :]
                 )
             quantised[index] = (z_codes, z_scales)
 
-        def multiply(index):
+        def multiply(index, halves):
             first, count = groups[index]
             z_codes, z_scales = quantised[index]
             for r in range(count):
-                result = results.tile([P, FEATURES], F32)
-                for h in range(N_TILES):
+                if first + r not in row_results:
+                    result = results.tile([P, FEATURES], F32)
+                    row_results[first + r] = result
+                result = row_results[first + r]
+                for h in halves:
                     cols = slice(h * N_TILE, (h + 1) * N_TILE)
                     acc = sums.tile([P, N_TILE], F32, tag="acc")
                     for g in range(PASSES):
@@ -188,12 +185,53 @@ def tile_attention_pa_kernel(tc, y_attn, w_proj, b_proj, out):
                         nc.gpsimd.tensor_tensor(out=result[:, cols], in0=result[:, cols], in1=bias[:, cols], op=ADD)
                     else:
                         nc.vector.tensor_tensor(out=result[:, cols], in0=acc[:], in1=bias[:, cols], op=ADD)
-                nc.sync.dma_start(out=out_rows[:, first + r, :], in_=result[:])
+                if halves[-1] == N_TILES - 1:
+                    nc.sync.dma_start(out=out_rows[:, first + r, :], in_=result[:])
 
-        for step in range(-(LEAD + AHEAD), len(groups)):
-            if 0 <= step + LEAD < len(groups):
-                prepare(step + LEAD)
-            if step >= 0:
-                multiply(step)
-            if step + LEAD + AHEAD < len(groups):
-                interleave(step + LEAD + AHEAD, step < 0)
+        for t in range(HALF_W):
+            prepare_w(t)
+        quantise_w(0, HALF_W)
+
+        bias = keep.tile([P, FEATURES], F32)
+        for h in range(N_TILES):
+            cols = slice(h * N_TILE, (h + 1) * N_TILE)
+            spread = sums.tile([P, N_TILE], F32, tag="acc")
+            nc.tensor.matmul(out=spread[:], lhsT=ones[:], rhs=bias_rows[:, cols], start=True, stop=True)
+            nc.vector.tensor_copy(out=bias[:, cols], in_=spread[:])
+
+        interleave("vector", 0, 0, 144)
+        interleave("scalar", 0, 144, CHUNK)
+        interleave("vector", 1, reach[0], reach[1])
+        interleave("scalar", 1, reach[1], reach[2])
+        interleave("vector", 1, reach[2], reach[3])
+        transpose_rows(0, ("vector", "scalar"))
+        transpose_rows(1, ("scalar", "scalar"))
+        interleave("vector", 1, reach[3], reach[4])
+        quantise(0)
+        prepare_w(4)
+        prepare_w(5)
+        quantise(1)
+        multiply(0, (0,))
+        prepare_w(6)
+        prepare_w(7)
+        quantise_w(4, 4)
+        interleave("vector", 1, reach[4], reach[5])
+        multiply(1, (0,))
+        transpose_rows(2, ("scalar", "scalar"))
+        multiply(0, (1,))
+        quantise(2)
+        multiply(1, (1,))
+        interleave("vector", 1, reach[5], CHUNK)
+
+        for step in range(2, len(groups)):
+            if step + 1 < len(groups):
+                transpose_rows(step + 1, ("scalar", "scalar"))
+                quantise(step + 1)
+            multiply(step, (0, 1))
+            if 6 <= step + 4 < len(groups):
+                interleave("scalar", 0, max(CHUNK, reach[step + 4]), reach[step + 5])
+            if 6 <= step + 3 < len(groups):
+                lo = max(CHUNK, reach[step + 3])
+                split = min(lo + SLAB, reach[step + 4])
+                interleave("gpsimd", 1, lo, split)
+                interleave("vector", 1, split, reach[step + 4])

@@ -31,7 +31,14 @@ HALF_W = W_TILES // N_TILES
 GROUP = 2
 RUN = 4
 SLAB = 16
-CHUNK = 256
+SPLIT = 192
+ODD_LEAD = 2
+EVEN_LEAD = 3
+G_PART = (16, 16)
+G_PIECE = 8
+V_PART = (0, 0)
+FIRST_LATE = 4
+Q_SLOT = 0
 RESULT_ROWS = 10
 
 FLOPS = 2 * IMAGES * TOKENS * K * FEATURES
@@ -65,20 +72,20 @@ def tile_attention_pa_kernel(tc, y_attn, w_proj, b_proj, out):
         def load_w(first, count):
             nc.sync.dma_start(out=w_raw[:, first : first + count, :], in_=w_tiles[:, first : first + count, :])
 
-        def load_y(c):
-            y_chunk = keep.tile([P, PARITIES, PAIRS, CHUNK], BF16, name="y_chunk%d" % c)
+        def load_y(first, width):
+            y_chunk = keep.tile([P, PARITIES, PAIRS, width], BF16, name="y_chunk%d" % len(y_chunks))
             for u in range(PARITIES):
                 for a in range(HALVES):
-                    lo = a * HALF_CHANNELS + c * CHUNK
-                    nc.sync.dma_start(out=y_chunk[a:P:HALVES, u, :, :], in_=y_tokens[:, u, :, lo : lo + CHUNK])
-            y_chunks.append(y_chunk)
+                    lo = a * HALF_CHANNELS + first
+                    nc.sync.dma_start(out=y_chunk[a:P:HALVES, u, :, :], in_=y_tokens[:, u, :, lo : lo + width])
+            y_chunks.append((y_chunk, first))
 
         load_w(0, HALF_W)
         nc.sync.dma_start(out=bias_rows[0:1, :], in_=b_proj.rearrange("(o f) -> o f", o=1))
-        load_y(0)
+        load_y(0, SPLIT)
         load_w(HALF_W, HALF_W // 2)
         load_w(HALF_W + HALF_W // 2, HALF_W // 2)
-        load_y(1)
+        load_y(SPLIT, HALF_CHANNELS - SPLIT)
 
         w_grouped = keep.tile([P, PASSES, FEATURES * PACK], BF16, align_bytes=64)
         w_codes = keep.tile([P, PASSES, FEATURES], U32, align_bytes=64)
@@ -112,17 +119,18 @@ def tile_attention_pa_kernel(tc, y_attn, w_proj, b_proj, out):
         reach = [0] + [channels_through(first + count) for first, count in groups]
         quantised = {}
         row_results = {}
+        row_results = {}
 
         def interleave(engine, u, lo, hi):
             if lo >= hi:
                 return
-            c = lo // CHUNK
-            if hi > (c + 1) * CHUNK:
-                interleave(engine, u, lo, (c + 1) * CHUNK)
-                interleave(engine, u, (c + 1) * CHUNK, hi)
+            if lo < SPLIT < hi:
+                interleave(engine, u, lo, SPLIT)
+                interleave(engine, u, SPLIT, hi)
                 return
+            y_chunk, first = y_chunks[lo >= SPLIT]
             dst = z_planes[:, u, PAIRS * lo : PAIRS * hi].rearrange("p (c i m) -> p c m i", i=RUN, m=PAIRS)
-            src = y_chunks[c][:, u, :, lo - c * CHUNK : hi - c * CHUNK].rearrange("p m (c i) -> p c m i", i=RUN)
+            src = y_chunk[:, u, :, lo - first : hi - first].rearrange("p m (c i) -> p c m i", i=RUN)
             if engine == "vector":
                 nc.vector.tensor_copy(out=dst, in_=src)
             elif engine == "scalar":
@@ -130,7 +138,7 @@ def tile_attention_pa_kernel(tc, y_attn, w_proj, b_proj, out):
             else:
                 nc.gpsimd.tensor_scalar(out=dst, in0=src, scalar1=1.0, scalar2=0.0, op0=MULT, op1=ADD)
 
-        def transpose_rows(index, engines):
+        def transpose_rows(index):
             first, count = groups[index]
             z_grouped = zq.tile([P, GROUP, PASSES * P * PACK], BF16, align_bytes=64)
             for r in range(count):
@@ -142,26 +150,22 @@ def tile_attention_pa_kernel(tc, y_attn, w_proj, b_proj, out):
                     nc.tensor.transpose(bank[:, v, :], words, identity[:])
                 target = z_grouped[:, r, :].bitcast(F32).rearrange("p (g r u) -> p g r u", g=PASSES, u=2)
                 source = bank[:].rearrange("p (g u) r -> p g r u", g=PASSES)
-                if engines[r] == "vector":
-                    nc.vector.tensor_copy(out=target, in_=source)
-                else:
-                    nc.scalar.copy(out=target, in_=source)
-            quantised[index] = [z_grouped]
-
-        def quantise(index):
-            first, count = groups[index]
-            z_grouped = quantised[index][0]
+                nc.scalar.copy(out=target, in_=source)
             z_codes = zq.tile([P, GROUP, PASSES * P], U32, align_bytes=64)
             z_scales = zq.tile([P, GROUP, PASSES * P], U8, align_bytes=64)
-            for r in range(count):
-                nc.vector.quantize_mx(
-                    out=z_codes[:, r, :].bitcast(FP8X4), scales=z_scales[:, r, :], in_=z_grouped[:, r, :]
-                )
-            quantised[index] = (z_codes, z_scales)
+            quantised[index] = (z_grouped, z_codes, z_scales)
 
-        def multiply(index, halves):
+        def quantise(index, rows):
+            z_grouped, z_codes, z_scales = quantised[index]
+            nc.vector.quantize_mx(
+                out=z_codes[:, rows, :].rearrange("p r c -> p (r c)").bitcast(FP8X4),
+                scales=z_scales[:, rows, :].rearrange("p r c -> p (r c)"),
+                in_=z_grouped[:, rows, :].rearrange("p r c -> p (r c)"),
+            )
+
+        def multiply(index, halves, between):
             first, count = groups[index]
-            z_codes, z_scales = quantised[index]
+            z_codes, z_scales = quantised[index][1:]
             for r in range(count):
                 if first + r not in row_results:
                     result = results.tile([P, FEATURES], F32)
@@ -180,11 +184,9 @@ def tile_attention_pa_kernel(tc, y_attn, w_proj, b_proj, out):
                             start=(g == 0),
                             stop=(g == PASSES - 1),
                         )
-                    if r == 1 and h == 0:
-                        nc.scalar.copy(out=result[:, cols], in_=acc[:])
-                        nc.gpsimd.tensor_tensor(out=result[:, cols], in0=result[:, cols], in1=bias[:, cols], op=ADD)
-                    else:
-                        nc.vector.tensor_tensor(out=result[:, cols], in0=acc[:], in1=bias[:, cols], op=ADD)
+                    nc.vector.tensor_tensor(out=result[:, cols], in0=acc[:], in1=bias[:, cols], op=ADD)
+                    if between:
+                        between.pop(0)()
                 if halves[-1] == N_TILES - 1:
                     nc.sync.dma_start(out=out_rows[:, first + r, :], in_=result[:])
 
@@ -199,39 +201,57 @@ def tile_attention_pa_kernel(tc, y_attn, w_proj, b_proj, out):
             nc.tensor.matmul(out=spread[:], lhsT=ones[:], rhs=bias_rows[:, cols], start=True, stop=True)
             nc.vector.tensor_copy(out=bias[:, cols], in_=spread[:])
 
-        interleave("vector", 0, 0, 144)
-        interleave("scalar", 0, 144, CHUNK)
+        interleave("scalar", 0, 0, 64)
+        interleave("vector", 0, 64, SPLIT)
         interleave("vector", 1, reach[0], reach[1])
-        interleave("scalar", 1, reach[1], reach[2])
+        interleave("scalar", 1, reach[1], reach[1] + 32)
+        interleave("vector", 1, reach[1] + 32, reach[2])
+        transpose_rows(0)
+        transpose_rows(1)
         interleave("vector", 1, reach[2], reach[3])
-        transpose_rows(0, ("vector", "scalar"))
-        transpose_rows(1, ("scalar", "scalar"))
-        interleave("vector", 1, reach[3], reach[4])
-        quantise(0)
+        quantise(0, slice(0, 2))
         prepare_w(4)
         prepare_w(5)
-        quantise(1)
-        multiply(0, (0,))
+        quantise(1, slice(0, 2))
+        multiply(0, (0,), [])
         prepare_w(6)
         prepare_w(7)
         quantise_w(4, 4)
-        interleave("vector", 1, reach[4], reach[5])
-        multiply(1, (0,))
-        transpose_rows(2, ("scalar", "scalar"))
-        multiply(0, (1,))
-        quantise(2)
-        multiply(1, (1,))
-        interleave("vector", 1, reach[5], CHUNK)
+        multiply(1, (0,), [])
+        interleave("vector", 1, reach[3], min(SPLIT, reach[4]))
+        transpose_rows(2)
+        quantise(2, slice(0, 2))
+        multiply(0, (1,), [])
+        interleave("vector", 1, reach[4], max(reach[4], SPLIT))
+        multiply(1, (1,), [])
+
+        interleave("scalar", 0, SPLIT, reach[FIRST_LATE + 1])
 
         for step in range(2, len(groups)):
-            if step + 1 < len(groups):
-                transpose_rows(step + 1, ("scalar", "scalar"))
-                quantise(step + 1)
-            multiply(step, (0, 1))
-            if 6 <= step + 4 < len(groups):
-                interleave("scalar", 0, max(CHUNK, reach[step + 4]), reach[step + 5])
-            if 6 <= step + 3 < len(groups):
-                lo = max(CHUNK, reach[step + 3])
-                split = min(lo + SLAB, reach[step + 4])
-                interleave("gpsimd", 1, lo, split)
-                interleave("vector", 1, split, reach[step + 4])
+            ahead = groups[step + 1][1] if step + 1 < len(groups) else 0
+
+            def nothing():
+                pass
+
+            def quantise_next():
+                if ahead:
+                    quantise(step + 1, slice(0, ahead))
+
+            def interleave_later():
+                for u, lead in ((1, ODD_LEAD), (0, EVEN_LEAD)):
+                    index = step + lead
+                    if FIRST_LATE <= index < len(groups):
+                        lo, hi = max(SPLIT, reach[index]), reach[index + 1]
+                        v_end = min(hi, lo + V_PART[u])
+                        g_end = min(hi, v_end + G_PART[u])
+                        interleave("vector", u, lo, v_end)
+                        for part in range(v_end, g_end, G_PIECE):
+                            interleave("gpsimd", u, part, min(part + G_PIECE, g_end))
+                        interleave("scalar", u, g_end, hi)
+
+            if ahead:
+                transpose_rows(step + 1)
+            slots = [nothing, nothing, nothing, nothing]
+            slots[Q_SLOT] = quantise_next
+            multiply(step, (0, 1), slots)
+            interleave_later()

@@ -97,9 +97,9 @@ def tile_attention_pa_kernel(tc, y_attn, w_proj, b_proj, out):
             for v in range(BANK_PLANES):
                 g, x = divmod(v, 2)
                 nc.tensor.transpose(bank[:, v, :], words[:, g * 2 * P + x : (g + 1) * 2 * P : 2], identity[:])
-            target = w_grouped[:, :, t * P * PACK : (t + 1) * P * PACK].rearrange("p g (r y x) -> p g r y x", y=2, x=2)
+            target = w_grouped[:, :, t * P * PACK : (t + 1) * P * PACK].rearrange("p g (r y x) -> p g r x y", y=2, x=2)
             source = bank[:].rearrange("p v r -> p (v r)").bitcast(BF16)
-            source = source.rearrange("p (g x r y) -> p g r y x", g=PASSES, x=2, y=2)
+            source = source.rearrange("p (g x r y) -> p g r x y", g=PASSES, x=2, y=2)
             for g in range(PASSES):
                 if t % 2 == 0:
                     nc.vector.tensor_copy(out=target[:, g], in_=source[:, g])

@@ -15,47 +15,42 @@ TOKENS = 50
 CHANNELS = 1024
 FEATURES = 1024
 K = 1024
-HALVES = 2
-HALF_CHANNELS = CHANNELS // HALVES
-ROWS = TOKENS // HALVES
 PARITIES = 2
 PAIRS = TOKENS // PARITIES
 PACK = 4
 K_PASS = P * PACK
 PASSES = K // K_PASS
-BANK_PLANES = PASSES * 2
+TILE_ROWS = P // IMAGES
+TILES = TOKENS // TILE_ROWS
 N_TILE = 512
 N_TILES = FEATURES // N_TILE
 W_TILES = FEATURES // P
 HALF_W = W_TILES // N_TILES
-GROUP = 2
+GROUPS = (1,) + (2,) * 12
+GROUP_MAX = max(GROUPS)
 RUN = 4
 SLAB = 16
-SPLIT = 192
-ODD_LEAD = 2
-EVEN_LEAD = 3
-G_PART = (16, 16)
-G_PIECE = 8
-V_PART = (0, 0)
-FIRST_LATE = 4
+CHUNKS = (256, 256, 512)
+LEAD = 3
+V_FIRST = 224
+SHARES = (("gpsimd", 32, 8), ("scalar", None, 64))
 Q_SLOT = 0
-RESULT_ROWS = 10
+RESULT_TILES = 10
 
 FLOPS = 2 * IMAGES * TOKENS * K * FEATURES
 
 
-def channels_through(rows):
-    return min(HALF_CHANNELS, -(-rows * K // (TOKENS * SLAB)) * SLAB)
+def channels_through(tiles):
+    return min(CHANNELS, -(-tiles * TILE_ROWS * K // (TOKENS * SLAB)) * SLAB)
 
 
 def tile_attention_pa_kernel(tc, y_attn, w_proj, b_proj, out):
     nc = tc.nc
-    out_rows = out.rearrange("b (a i) f -> (b a) i f", a=HALVES)
     w_tiles = w_proj.rearrange("(t p) j -> p t j", p=P)
     y_tokens = y_attn.rearrange("b (m u) c -> b u m c", u=PARITIES)
 
     with tc.tile_pool(name="keep", bufs=1) as keep, tc.tile_pool(name="zq", bufs=4) as zq, tc.tile_pool(
-        name="results", bufs=RESULT_ROWS
+        name="results", bufs=RESULT_TILES
     ) as results, tc.psum_pool(name="planes", bufs=4) as planes, tc.psum_pool(
         name="sums", bufs=4
     ) as sums, tc.manual_schedule():
@@ -73,28 +68,32 @@ def tile_attention_pa_kernel(tc, y_attn, w_proj, b_proj, out):
             nc.sync.dma_start(out=w_raw[:, first : first + count, :], in_=w_tiles[:, first : first + count, :])
 
         def load_y(first, width):
-            y_chunk = keep.tile([P, PARITIES, PAIRS, width], BF16, name="y_chunk%d" % len(y_chunks))
+            y_chunk = keep.tile([P, PAIRS, width], BF16, name="y_chunk%d" % len(y_chunks))
             for u in range(PARITIES):
-                for a in range(HALVES):
-                    lo = a * HALF_CHANNELS + first
-                    nc.sync.dma_start(out=y_chunk[a:P:HALVES, u, :, :], in_=y_tokens[:, u, :, lo : lo + width])
-            y_chunks.append((y_chunk, first))
+                nc.sync.dma_start(out=y_chunk[u:P:PARITIES, :, :], in_=y_tokens[:, u, :, first : first + width])
+            y_chunks.append((y_chunk, first, width))
 
-        load_w(0, HALF_W)
         nc.sync.dma_start(out=bias_rows[0:1, :], in_=b_proj.rearrange("(o f) -> o f", o=1))
-        load_y(0, SPLIT)
-        load_w(HALF_W, HALF_W // 2)
-        load_w(HALF_W + HALF_W // 2, HALF_W // 2)
-        load_y(SPLIT, HALF_CHANNELS - SPLIT)
+        for h in range(N_TILES):
+            load_w(h * HALF_W, HALF_W)
+        for c in range(len(CHUNKS)):
+            load_y(sum(CHUNKS[:c]), CHUNKS[c])
+
+        bias = keep.tile([P, FEATURES], F32)
+        for h in range(N_TILES):
+            cols = slice(h * N_TILE, (h + 1) * N_TILE)
+            spread = sums.tile([P, N_TILE], F32, tag="acc")
+            nc.tensor.matmul(out=spread[:], lhsT=ones[:], rhs=bias_rows[:, cols], start=True, stop=True)
+            nc.vector.tensor_copy(out=bias[:, cols], in_=spread[:])
 
         w_grouped = keep.tile([P, PASSES, FEATURES * PACK], BF16, align_bytes=64)
         w_codes = keep.tile([P, PASSES, FEATURES], U32, align_bytes=64)
         w_scales = keep.tile([P, PASSES, FEATURES], U8, align_bytes=64)
 
         def prepare_w(t):
-            bank = planes.tile([P, BANK_PLANES, P], F32, tag="bank")
+            bank = planes.tile([P, PASSES * 2, P], F32, tag="bank")
             words = w_raw[:, t, :].bitcast(F32)
-            for v in range(BANK_PLANES):
+            for v in range(PASSES * 2):
                 g, x = divmod(v, 2)
                 nc.tensor.transpose(bank[:, v, :], words[:, g * 2 * P + x : (g + 1) * 2 * P : 2], identity[:])
             target = w_grouped[:, :, t * P * PACK : (t + 1) * P * PACK].rearrange("p g (r y x) -> p g r x y", y=2, x=2)
@@ -114,71 +113,72 @@ def tile_attention_pa_kernel(tc, y_attn, w_proj, b_proj, out):
                     in_=w_grouped[:, g, first * P * PACK : (first + count) * P * PACK],
                 )
 
-        z_planes = keep.tile([P, PARITIES, ROWS * K // PARITIES], BF16, align_bytes=64)
-        groups = [(first, min(GROUP, ROWS - first)) for first in range(0, ROWS, GROUP)]
+        z_stream = keep.tile([P, PAIRS * CHANNELS], BF16, align_bytes=64)
+        groups = [(sum(GROUPS[:s]), GROUPS[s]) for s in range(len(GROUPS))]
         reach = [0] + [channels_through(first + count) for first, count in groups]
         quantised = {}
-        row_results = {}
-        row_results = {}
+        tile_results = {}
 
-        def interleave(engine, u, lo, hi):
-            if lo >= hi:
-                return
-            if lo < SPLIT < hi:
-                interleave(engine, u, lo, SPLIT)
-                interleave(engine, u, SPLIT, hi)
-                return
-            y_chunk, first = y_chunks[lo >= SPLIT]
-            dst = z_planes[:, u, PAIRS * lo : PAIRS * hi].rearrange("p (c i m) -> p c m i", i=RUN, m=PAIRS)
-            src = y_chunk[:, u, :, lo - first : hi - first].rearrange("p m (c i) -> p c m i", i=RUN)
-            if engine == "vector":
-                nc.vector.tensor_copy(out=dst, in_=src)
-            elif engine == "scalar":
-                nc.scalar.copy(out=dst, in_=src)
-            else:
-                nc.gpsimd.tensor_scalar(out=dst, in0=src, scalar1=1.0, scalar2=0.0, op0=MULT, op1=ADD)
+        def interleave(engine, lo, hi):
+            for y_chunk, first, width in y_chunks:
+                begin, end = max(lo, first), min(hi, first + width)
+                if begin < end:
+                    dst = z_stream[:, PAIRS * begin : PAIRS * end].rearrange("p (c i m) -> p c m i", i=RUN, m=PAIRS)
+                    src = y_chunk[:, :, begin - first : end - first].rearrange("p m (c i) -> p c m i", i=RUN)
+                    if engine == "vector":
+                        nc.vector.tensor_copy(out=dst, in_=src)
+                    elif engine == "scalar":
+                        nc.scalar.copy(out=dst, in_=src)
+                    else:
+                        nc.gpsimd.tensor_scalar(out=dst, in0=src, scalar1=1.0, scalar2=0.0, op0=MULT, op1=ADD)
 
-        def transpose_rows(index):
+        def transpose_tiles(index):
             first, count = groups[index]
-            z_grouped = zq.tile([P, GROUP, PASSES * P * PACK], BF16, align_bytes=64)
-            for r in range(count):
-                bank = planes.tile([P, BANK_PLANES, P], F32, tag="bank")
-                for v in range(BANK_PLANES):
-                    g, u = divmod(v, 2)
-                    start = ((first + r) * K + g * K_PASS) // PARITIES
-                    words = z_planes[:, u, start : start + K_PASS // PARITIES].bitcast(F32)
+            z_grouped = zq.tile([P, GROUP_MAX, PASSES * P * PACK], BF16, align_bytes=64)
+            for k in range(count):
+                bank = planes.tile([P, TILE_ROWS * PASSES, P], F32, tag="bank")
+                for v in range(TILE_ROWS * PASSES):
+                    r, g = divmod(v, PASSES)
+                    start = (((first + k) * TILE_ROWS + r) * K + g * K_PASS) // PARITIES
+                    words = z_stream[:, start : start + K_PASS // PARITIES].bitcast(F32)
                     nc.tensor.transpose(bank[:, v, :], words, identity[:])
-                target = z_grouped[:, r, :].bitcast(F32).rearrange("p (g r u) -> p g r u", g=PASSES, u=2)
-                source = bank[:].rearrange("p (g u) r -> p g r u", g=PASSES)
+                target = z_grouped[:, k, :].bitcast(F32)
+                target = target.rearrange("p (g b r u) -> p g b r u", g=PASSES, b=IMAGES, r=TILE_ROWS)
+                source = bank[:].rearrange("p (r g) (b u) -> p g b r u", r=TILE_ROWS, u=PARITIES)
                 nc.scalar.copy(out=target, in_=source)
-            z_codes = zq.tile([P, GROUP, PASSES * P], U32, align_bytes=64)
-            z_scales = zq.tile([P, GROUP, PASSES * P], U8, align_bytes=64)
+            z_codes = zq.tile([P, GROUP_MAX, PASSES * P], U32, align_bytes=64)
+            z_scales = zq.tile([P, GROUP_MAX, PASSES * P], U8, align_bytes=64)
             quantised[index] = (z_grouped, z_codes, z_scales)
 
-        def quantise(index, rows):
+        def quantise(index):
             z_grouped, z_codes, z_scales = quantised[index]
+            count = groups[index][1]
             nc.vector.quantize_mx(
-                out=z_codes[:, rows, :].rearrange("p r c -> p (r c)").bitcast(FP8X4),
-                scales=z_scales[:, rows, :].rearrange("p r c -> p (r c)"),
-                in_=z_grouped[:, rows, :].rearrange("p r c -> p (r c)"),
+                out=z_codes[:, 0:count, :].rearrange("p k c -> p (k c)").bitcast(FP8X4),
+                scales=z_scales[:, 0:count, :].rearrange("p k c -> p (k c)"),
+                in_=z_grouped[:, 0:count, :].rearrange("p k c -> p (k c)"),
             )
+
+        def store(tile, result, cols):
+            for r in range(TILE_ROWS):
+                nc.sync.dma_start(out=out[:, tile * TILE_ROWS + r, cols], in_=result[r:P:TILE_ROWS, cols])
 
         def multiply(index, halves, between):
             first, count = groups[index]
             z_codes, z_scales = quantised[index][1:]
-            for r in range(count):
-                if first + r not in row_results:
+            for k in range(count):
+                if first + k not in tile_results:
                     result = results.tile([P, FEATURES], F32)
-                    row_results[first + r] = result
-                result = row_results[first + r]
+                    tile_results[first + k] = result
+                result = tile_results[first + k]
                 for h in halves:
                     cols = slice(h * N_TILE, (h + 1) * N_TILE)
                     acc = sums.tile([P, N_TILE], F32, tag="acc")
                     for g in range(PASSES):
                         nc.tensor.matmul_mx(
                             out=acc[:],
-                            lhsT=z_codes[:, r, g * P : (g + 1) * P].bitcast(FP8X4),
-                            lhsT_scale=z_scales[:, r, g * P : (g + 1) * P],
+                            lhsT=z_codes[:, k, g * P : (g + 1) * P].bitcast(FP8X4),
+                            lhsT_scale=z_scales[:, k, g * P : (g + 1) * P],
                             rhs=w_codes[:, g, cols].bitcast(FP8X4),
                             rhs_scale=w_scales[:, g, cols],
                             start=(g == 0),
@@ -187,71 +187,50 @@ def tile_attention_pa_kernel(tc, y_attn, w_proj, b_proj, out):
                     nc.vector.tensor_tensor(out=result[:, cols], in0=acc[:], in1=bias[:, cols], op=ADD)
                     if between:
                         between.pop(0)()
-                if halves[-1] == N_TILES - 1:
-                    nc.sync.dma_start(out=out_rows[:, first + r, :], in_=result[:])
+                    if first + k == TILES - 1:
+                        store(first + k, result, cols)
+                if first + k < TILES - 1:
+                    store(first + k, result, slice(0, FEATURES))
 
-        for t in range(HALF_W):
+        for t in range(W_TILES):
             prepare_w(t)
-        quantise_w(0, HALF_W)
+            if t % 2 == 1 and t < W_TILES - 1:
+                quantise_w(t - 1, 2)
+        covered = [0]
 
-        bias = keep.tile([P, FEATURES], F32)
-        for h in range(N_TILES):
-            cols = slice(h * N_TILE, (h + 1) * N_TILE)
-            spread = sums.tile([P, N_TILE], F32, tag="acc")
-            nc.tensor.matmul(out=spread[:], lhsT=ones[:], rhs=bias_rows[:, cols], start=True, stop=True)
-            nc.vector.tensor_copy(out=bias[:, cols], in_=spread[:])
+        def interleave_through(index, shares):
+            lo, end = covered[0], reach[min(index, len(groups))]
+            for engine, count, piece in shares:
+                hi = end if count is None else min(end, lo + count)
+                for begin in range(lo, hi, piece):
+                    interleave(engine, begin, min(begin + piece, hi))
+                lo = max(lo, hi)
+            covered[0] = max(covered[0], end)
 
-        interleave("scalar", 0, 0, 64)
-        interleave("vector", 0, 64, SPLIT)
-        interleave("vector", 1, reach[0], reach[1])
-        interleave("scalar", 1, reach[1], reach[1] + 32)
-        interleave("vector", 1, reach[1] + 32, reach[2])
-        transpose_rows(0)
-        transpose_rows(1)
-        interleave("vector", 1, reach[2], reach[3])
-        quantise(0, slice(0, 2))
-        prepare_w(4)
-        prepare_w(5)
-        quantise(1, slice(0, 2))
-        multiply(0, (0,), [])
-        prepare_w(6)
-        prepare_w(7)
-        quantise_w(4, 4)
-        multiply(1, (0,), [])
-        interleave("vector", 1, reach[3], min(SPLIT, reach[4]))
-        transpose_rows(2)
-        quantise(2, slice(0, 2))
-        multiply(0, (1,), [])
-        interleave("vector", 1, reach[4], max(reach[4], SPLIT))
-        multiply(1, (1,), [])
+        interleave("vector", 0, 48)
+        interleave("scalar", 48, 80)
+        quantise_w(W_TILES - 2, 2)
+        transpose_tiles(0)
+        interleave("vector", 80, 128)
+        transpose_tiles(1)
+        quantise(0)
+        interleave("vector", 128, V_FIRST)
+        interleave("scalar", V_FIRST, CHUNKS[0])
+        covered[0] = CHUNKS[0]
 
-        interleave("scalar", 0, SPLIT, reach[FIRST_LATE + 1])
-
-        for step in range(2, len(groups)):
-            ahead = groups[step + 1][1] if step + 1 < len(groups) else 0
+        for step in range(len(groups)):
+            ahead = step + 1 < len(groups)
 
             def nothing():
                 pass
 
             def quantise_next():
                 if ahead:
-                    quantise(step + 1, slice(0, ahead))
+                    quantise(step + 1)
 
-            def interleave_later():
-                for u, lead in ((1, ODD_LEAD), (0, EVEN_LEAD)):
-                    index = step + lead
-                    if FIRST_LATE <= index < len(groups):
-                        lo, hi = max(SPLIT, reach[index]), reach[index + 1]
-                        v_end = min(hi, lo + V_PART[u])
-                        g_end = min(hi, v_end + G_PART[u])
-                        interleave("vector", u, lo, v_end)
-                        for part in range(v_end, g_end, G_PIECE):
-                            interleave("gpsimd", u, part, min(part + G_PIECE, g_end))
-                        interleave("scalar", u, g_end, hi)
-
-            if ahead:
-                transpose_rows(step + 1)
-            slots = [nothing, nothing, nothing, nothing]
+            if ahead and step > 0:
+                transpose_tiles(step + 1)
+            slots = [nothing] * (2 * GROUP_MAX)
             slots[Q_SLOT] = quantise_next
             multiply(step, (0, 1), slots)
-            interleave_later()
+            interleave_through(step + LEAD + 1, SHARES)

@@ -136,16 +136,13 @@ def tile_attention_pa_kernel(tc, y_attn, w_proj, b_proj, out):
             first, count = groups[index]
             z_grouped = zq.tile([P, GROUP_MAX, PASSES * P * PACK], BF16, align_bytes=64)
             for k in range(count):
-                bank = planes.tile([P, TILE_ROWS * PASSES, P], F32, tag="bank")
+                bank = planes.tile([P, PASSES, IMAGES, TILE_ROWS * PARITIES], F32, tag="bank")
                 for v in range(TILE_ROWS * PASSES):
                     r, g = divmod(v, PASSES)
                     start = (((first + k) * TILE_ROWS + r) * K + g * K_PASS) // PARITIES
                     words = z_stream[:, start : start + K_PASS // PARITIES].bitcast(F32)
-                    nc.tensor.transpose(bank[:, v, :], words, identity[:])
-                target = z_grouped[:, k, :].bitcast(F32)
-                target = target.rearrange("p (g b r u) -> p g b r u", g=PASSES, b=IMAGES, r=TILE_ROWS)
-                source = bank[:].rearrange("p (r g) (b u) -> p g b r u", r=TILE_ROWS, u=PARITIES)
-                nc.scalar.copy(out=target, in_=source)
+                    nc.tensor.transpose(bank[:, g, :, r * PARITIES : (r + 1) * PARITIES], words, identity[:])
+                nc.scalar.copy(out=z_grouped[:, k, :].bitcast(F32), in_=bank[:].rearrange("p g b x -> p (g b x)"))
             z_codes = zq.tile([P, GROUP_MAX, PASSES * P], U32, align_bytes=64)
             z_scales = zq.tile([P, GROUP_MAX, PASSES * P], U8, align_bytes=64)
             quantised[index] = (z_grouped, z_codes, z_scales)

@@ -35,7 +35,7 @@ LEAD = 3
 V_FIRST = 224
 SHARES = (("gpsimd", 32, 8), ("scalar", None, 64))
 Q_SLOT = 0
-RESULT_TILES = 10
+RESULT_GROUPS = 5
 
 FLOPS = 2 * IMAGES * TOKENS * K * FEATURES
 
@@ -50,7 +50,7 @@ def tile_attention_pa_kernel(tc, y_attn, w_proj, b_proj, out):
     y_tokens = y_attn.rearrange("b (m u) c -> b u m c", u=PARITIES)
 
     with tc.tile_pool(name="keep", bufs=1) as keep, tc.tile_pool(name="zq", bufs=4) as zq, tc.tile_pool(
-        name="results", bufs=RESULT_TILES
+        name="results", bufs=RESULT_GROUPS
     ) as results, tc.psum_pool(name="planes", bufs=4) as planes, tc.psum_pool(
         name="sums", bufs=4
     ) as sums, tc.manual_schedule():
@@ -117,7 +117,10 @@ def tile_attention_pa_kernel(tc, y_attn, w_proj, b_proj, out):
         groups = [(sum(GROUPS[:s]), GROUPS[s]) for s in range(len(GROUPS))]
         reach = [0] + [channels_through(first + count) for first, count in groups]
         quantised = {}
-        tile_results = {}
+
+        def row_of(index, k, r):
+            first, count = groups[index]
+            return first * TILE_ROWS + r * count + k
 
         def interleave(engine, lo, hi):
             for y_chunk, first, width in y_chunks:
@@ -139,7 +142,7 @@ def tile_attention_pa_kernel(tc, y_attn, w_proj, b_proj, out):
                 bank = planes.tile([P, PASSES, IMAGES, TILE_ROWS * PARITIES], F32, tag="bank")
                 for v in range(TILE_ROWS * PASSES):
                     r, g = divmod(v, PASSES)
-                    start = (((first + k) * TILE_ROWS + r) * K + g * K_PASS) // PARITIES
+                    start = (row_of(index, k, r) * K + g * K_PASS) // PARITIES
                     words = z_stream[:, start : start + K_PASS // PARITIES].bitcast(F32)
                     nc.tensor.transpose(bank[:, g, :, r * PARITIES : (r + 1) * PARITIES], words, identity[:])
                 nc.scalar.copy(out=z_grouped[:, k, :].bitcast(F32), in_=bank[:].rearrange("p g b x -> p (g b x)"))
@@ -156,19 +159,19 @@ def tile_attention_pa_kernel(tc, y_attn, w_proj, b_proj, out):
                 in_=z_grouped[:, 0:count, :].rearrange("p k c -> p (k c)"),
             )
 
-        def store(tile, result, cols):
+        def store(index, k, count, result, cols):
             for r in range(TILE_ROWS):
-                nc.sync.dma_start(out=out[:, tile * TILE_ROWS + r, cols], in_=result[r:P:TILE_ROWS, cols])
+                row = row_of(index, k, r)
+                nc.sync.dma_start(
+                    out=out[:, row : row + count, cols], in_=result[r:P:TILE_ROWS, k : k + count, cols]
+                )
 
-        def multiply(index, halves, between):
+        def multiply(index, between):
             first, count = groups[index]
             z_codes, z_scales = quantised[index][1:]
+            result = results.tile([P, GROUP_MAX, FEATURES], F32)
             for k in range(count):
-                if first + k not in tile_results:
-                    result = results.tile([P, FEATURES], F32)
-                    tile_results[first + k] = result
-                result = tile_results[first + k]
-                for h in halves:
+                for h in range(N_TILES):
                     cols = slice(h * N_TILE, (h + 1) * N_TILE)
                     acc = sums.tile([P, N_TILE], F32, tag="acc")
                     for g in range(PASSES):
@@ -181,13 +184,15 @@ def tile_attention_pa_kernel(tc, y_attn, w_proj, b_proj, out):
                             start=(g == 0),
                             stop=(g == PASSES - 1),
                         )
-                    nc.vector.tensor_tensor(out=result[:, cols], in0=acc[:], in1=bias[:, cols], op=ADD)
+                    nc.vector.tensor_tensor(out=result[:, k, cols], in0=acc[:], in1=bias[:, cols], op=ADD)
                     if between:
                         between.pop(0)()
                     if first + k == TILES - 1:
-                        store(first + k, result, cols)
-                if first + k < TILES - 1:
-                    store(first + k, result, slice(0, FEATURES))
+                        store(index, k, 1, result, cols)
+                if first + count == TILES and k < count - 1:
+                    store(index, k, 1, result, slice(0, FEATURES))
+            if first + count < TILES:
+                store(index, 0, count, result, slice(0, FEATURES))
 
         for t in range(W_TILES):
             prepare_w(t)
@@ -229,5 +234,5 @@ def tile_attention_pa_kernel(tc, y_attn, w_proj, b_proj, out):
                 transpose_tiles(step + 1)
             slots = [nothing] * (2 * GROUP_MAX)
             slots[Q_SLOT] = quantise_next
-            multiply(step, (0, 1), slots)
+            multiply(step, slots)
             interleave_through(step + LEAD + 1, SHARES)

@@ -31,10 +31,12 @@ GROUP_MAX = max(GROUPS)
 RUN = 4
 SLAB = 16
 CHUNKS = (256, 256, 512)
+WARM_UPS = 2
 LEAD = 3
 V_FIRST = 224
 SHARES = (("gpsimd", 32, 8), ("scalar", None, 64))
 Q_SLOT = 0
+SINGLE_STORES = 3
 RESULT_GROUPS = 5
 
 FLOPS = 2 * IMAGES * TOKENS * K * FEATURES
@@ -55,9 +57,11 @@ def tile_attention_pa_kernel(tc, y_attn, w_proj, b_proj, out):
         name="sums", bufs=4
     ) as sums, tc.manual_schedule():
         bias_rows = keep.tile([P, FEATURES], BF16)
-        nc.vector.memset(bias_rows[:], 0.0)
+        nc.gpsimd.memset(bias_rows[:].bitcast(U32), 0)
         ones = keep.tile([P, P], BF16)
         nc.vector.memset(ones[:], 1.0)
+        zeros = keep.tile([P, N_TILE], BF16)
+        nc.vector.memset(zeros[:].bitcast(U32), 0)
         identity = keep.tile([P, P], F32)
         make_identity(nc, identity[:])
 
@@ -80,6 +84,9 @@ def tile_attention_pa_kernel(tc, y_attn, w_proj, b_proj, out):
             load_y(sum(CHUNKS[:c]), CHUNKS[c])
 
         bias = keep.tile([P, FEATURES], F32)
+        for warm_up in range(WARM_UPS):
+            unread = sums.tile([P, N_TILE], F32, tag="acc")
+            nc.tensor.matmul(out=unread[:], lhsT=ones[:], rhs=zeros[:], start=True, stop=True)
         for h in range(N_TILES):
             cols = slice(h * N_TILE, (h + 1) * N_TILE)
             spread = sums.tile([P, N_TILE], F32, tag="acc")
@@ -170,6 +177,7 @@ def tile_attention_pa_kernel(tc, y_attn, w_proj, b_proj, out):
             first, count = groups[index]
             z_codes, z_scales = quantised[index][1:]
             result = results.tile([P, GROUP_MAX, FEATURES], F32)
+            singly = index >= len(groups) - SINGLE_STORES
             for k in range(count):
                 for h in range(N_TILES):
                     cols = slice(h * N_TILE, (h + 1) * N_TILE)
@@ -189,9 +197,9 @@ def tile_attention_pa_kernel(tc, y_attn, w_proj, b_proj, out):
                         between.pop(0)()
                     if first + k == TILES - 1:
                         store(index, k, 1, result, cols)
-                if first + count == TILES and k < count - 1:
+                if singly and first + k < TILES - 1:
                     store(index, k, 1, result, slice(0, FEATURES))
-            if first + count < TILES:
+            if not singly:
                 store(index, 0, count, result, slice(0, FEATURES))
 
         for t in range(W_TILES):

import concourse.mybir as mybir
from concourse.masks import make_identity

F32 = mybir.dt.float32
BF16 = mybir.dt.bfloat16
U32 = mybir.dt.uint32
U8 = mybir.dt.uint8
FP8X4 = mybir.dt.float8_e4m3fn_x4
ADD = mybir.AluOpType.add
MULT = mybir.AluOpType.mult

P = 128
IMAGES = 64
TOKENS = 50
CHANNELS = 1024
FEATURES = 1024
K = 1024
PARITIES = 2
PAIRS = TOKENS // PARITIES
PACK = 4
K_PASS = P * PACK
PASSES = K // K_PASS
TILE_ROWS = P // IMAGES
TILES = TOKENS // TILE_ROWS
N_TILE = 512
N_TILES = FEATURES // N_TILE
W_TILES = FEATURES // P
HALF_W = W_TILES // N_TILES
GROUPS = (1,) + (2,) * 12
GROUP_MAX = max(GROUPS)
RUN = 4
SLAB = 16
CHUNKS = (256, 256, 512)
WARM_UPS = 2
LEAD = 3
V_FIRST = 224
SHARES = (("gpsimd", 32, 8), ("scalar", None, 64))
Q_SLOT = 0
SINGLE_STORES = 3
RESULT_GROUPS = 5

FLOPS = 2 * IMAGES * TOKENS * K * FEATURES


def channels_through(tiles):
    return min(CHANNELS, -(-tiles * TILE_ROWS * K // (TOKENS * SLAB)) * SLAB)


def tile_attention_pa_kernel(tc, y_attn, w_proj, b_proj, out):
    nc = tc.nc
    w_tiles = w_proj.rearrange("(t p) j -> p t j", p=P)
    y_tokens = y_attn.rearrange("b (m u) c -> b u m c", u=PARITIES)

    with tc.tile_pool(name="keep", bufs=1) as keep, tc.tile_pool(name="zq", bufs=4) as zq, tc.tile_pool(
        name="results", bufs=RESULT_GROUPS
    ) as results, tc.psum_pool(name="planes", bufs=4) as planes, tc.psum_pool(
        name="sums", bufs=4
    ) as sums, tc.manual_schedule():
        bias_rows = keep.tile([P, FEATURES], BF16)
        nc.gpsimd.memset(bias_rows[:].bitcast(U32), 0)
        ones = keep.tile([P, P], BF16)
        nc.vector.memset(ones[:], 1.0)
        zeros = keep.tile([P, N_TILE], BF16)
        nc.vector.memset(zeros[:].bitcast(U32), 0)
        identity = keep.tile([P, P], F32)
        make_identity(nc, identity[:])

        w_raw = keep.tile([P, W_TILES, K], BF16)
        y_chunks = []

        def load_w(first, count):
            nc.sync.dma_start(out=w_raw[:, first : first + count, :], in_=w_tiles[:, first : first + count, :])

        def load_y(first, width):
            y_chunk = keep.tile([P, PAIRS, width], BF16, name="y_chunk%d" % len(y_chunks))
            for u in range(PARITIES):
                nc.sync.dma_start(out=y_chunk[u:P:PARITIES, :, :], in_=y_tokens[:, u, :, first : first + width])
            y_chunks.append((y_chunk, first, width))

        nc.sync.dma_start(out=bias_rows[0:1, :], in_=b_proj.rearrange("(o f) -> o f", o=1))
        for h in range(N_TILES):
            load_w(h * HALF_W, HALF_W)
        for c in range(len(CHUNKS)):
            load_y(sum(CHUNKS[:c]), CHUNKS[c])

        bias = keep.tile([P, FEATURES], F32)
        for warm_up in range(WARM_UPS):
            unread = sums.tile([P, N_TILE], F32, tag="acc")
            nc.tensor.matmul(out=unread[:], lhsT=ones[:], rhs=zeros[:], start=True, stop=True)
        for h in range(N_TILES):
            cols = slice(h * N_TILE, (h + 1) * N_TILE)
            spread = sums.tile([P, N_TILE], F32, tag="acc")
            nc.tensor.matmul(out=spread[:], lhsT=ones[:], rhs=bias_rows[:, cols], start=True, stop=True)
            nc.vector.tensor_copy(out=bias[:, cols], in_=spread[:])

        w_grouped = keep.tile([P, PASSES, FEATURES * PACK], BF16, align_bytes=64)
        w_codes = keep.tile([P, PASSES, FEATURES], U32, align_bytes=64)
        w_scales = keep.tile([P, PASSES, FEATURES], U8, align_bytes=64)

        def prepare_w(t):
            bank = planes.tile([P, PASSES * 2, P], F32, tag="bank")
            words = w_raw[:, t, :].bitcast(F32)
            for v in range(PASSES * 2):
                g, x = divmod(v, 2)
                nc.tensor.transpose(bank[:, v, :], words[:, g * 2 * P + x : (g + 1) * 2 * P : 2], identity[:])
            target = w_grouped[:, :, t * P * PACK : (t + 1) * P * PACK].rearrange("p g (r y x) -> p g r x y", y=2, x=2)
            source = bank[:].rearrange("p v r -> p (v r)").bitcast(BF16)
            source = source.rearrange("p (g x r y) -> p g r x y", g=PASSES, x=2, y=2)
            for g in range(PASSES):
                if t % 2 == 0:
                    nc.vector.tensor_copy(out=target[:, g], in_=source[:, g])
                else:
                    nc.scalar.copy(out=target[:, g], in_=source[:, g])

        def quantise_w(first, count):
            for g in range(PASSES):
                nc.vector.quantize_mx(
                    out=w_codes[:, g, first * P : (first + count) * P].bitcast(FP8X4),
                    scales=w_scales[:, g, first * P : (first + count) * P],
                    in_=w_grouped[:, g, first * P * PACK : (first + count) * P * PACK],
                )

        z_stream = keep.tile([P, PAIRS * CHANNELS], BF16, align_bytes=64)
        groups = [(sum(GROUPS[:s]), GROUPS[s]) for s in range(len(GROUPS))]
        reach = [0] + [channels_through(first + count) for first, count in groups]
        quantised = {}

        def row_of(index, k, r):
            first, count = groups[index]
            return first * TILE_ROWS + r * count + k

        def interleave(engine, lo, hi):
            for y_chunk, first, width in y_chunks:
                begin, end = max(lo, first), min(hi, first + width)
                if begin < end:
                    dst = z_stream[:, PAIRS * begin : PAIRS * end].rearrange("p (c i m) -> p c m i", i=RUN, m=PAIRS)
                    src = y_chunk[:, :, begin - first : end - first].rearrange("p m (c i) -> p c m i", i=RUN)
                    if engine == "vector":
                        nc.vector.tensor_copy(out=dst, in_=src)
                    elif engine == "scalar":
                        nc.scalar.copy(out=dst, in_=src)
                    else:
                        nc.gpsimd.tensor_scalar(out=dst, in0=src, scalar1=1.0, scalar2=0.0, op0=MULT, op1=ADD)

        def transpose_tiles(index):
            first, count = groups[index]
            z_grouped = zq.tile([P, GROUP_MAX, PASSES * P * PACK], BF16, align_bytes=64)
            for k in range(count):
                bank = planes.tile([P, PASSES, IMAGES, TILE_ROWS * PARITIES], F32, tag="bank")
                for v in range(TILE_ROWS * PASSES):
                    r, g = divmod(v, PASSES)
                    start = (row_of(index, k, r) * K + g * K_PASS) // PARITIES
                    words = z_stream[:, start : start + K_PASS // PARITIES].bitcast(F32)
                    nc.tensor.transpose(bank[:, g, :, r * PARITIES : (r + 1) * PARITIES], words, identity[:])
                nc.scalar.copy(out=z_grouped[:, k, :].bitcast(F32), in_=bank[:].rearrange("p g b x -> p (g b x)"))
            z_codes = zq.tile([P, GROUP_MAX, PASSES * P], U32, align_bytes=64)
            z_scales = zq.tile([P, GROUP_MAX, PASSES * P], U8, align_bytes=64)
            quantised[index] = (z_grouped, z_codes, z_scales)

        def quantise(index):
            z_grouped, z_codes, z_scales = quantised[index]
            count = groups[index][1]
            nc.vector.quantize_mx(
                out=z_codes[:, 0:count, :].rearrange("p k c -> p (k c)").bitcast(FP8X4),
                scales=z_scales[:, 0:count, :].rearrange("p k c -> p (k c)"),
                in_=z_grouped[:, 0:count, :].rearrange("p k c -> p (k c)"),
            )

        def store(index, k, count, result, cols):
            for r in range(TILE_ROWS):
                row = row_of(index, k, r)
                nc.sync.dma_start(
                    out=out[:, row : row + count, cols], in_=result[r:P:TILE_ROWS, k : k + count, cols]
                )

        def multiply(index, between):
            first, count = groups[index]
            z_codes, z_scales = quantised[index][1:]
            result = results.tile([P, GROUP_MAX, FEATURES], F32)
            singly = index >= len(groups) - SINGLE_STORES
            for k in range(count):
                for h in range(N_TILES):
                    cols = slice(h * N_TILE, (h + 1) * N_TILE)
                    acc = sums.tile([P, N_TILE], F32, tag="acc")
                    for g in range(PASSES):
                        nc.tensor.matmul_mx(
                            out=acc[:],
                            lhsT=z_codes[:, k, g * P : (g + 1) * P].bitcast(FP8X4),
                            lhsT_scale=z_scales[:, k, g * P : (g + 1) * P],
                            rhs=w_codes[:, g, cols].bitcast(FP8X4),
                            rhs_scale=w_scales[:, g, cols],
                            start=(g == 0),
                            stop=(g == PASSES - 1),
                        )
                    nc.vector.tensor_tensor(out=result[:, k, cols], in0=acc[:], in1=bias[:, cols], op=ADD)
                    if between:
                        between.pop(0)()
                    if first + k == TILES - 1:
                        store(index, k, 1, result, cols)
                if singly and first + k < TILES - 1:
                    store(index, k, 1, result, slice(0, FEATURES))
            if not singly:
                store(index, 0, count, result, slice(0, FEATURES))

        for t in range(W_TILES):
            prepare_w(t)
            if t % 2 == 1 and t < W_TILES - 1:
                quantise_w(t - 1, 2)
        covered = [0]

        def interleave_through(index, shares):
            lo, end = covered[0], reach[min(index, len(groups))]
            for engine, count, piece in shares:
                hi = end if count is None else min(end, lo + count)
                for begin in range(lo, hi, piece):
                    interleave(engine, begin, min(begin + piece, hi))
                lo = max(lo, hi)
            covered[0] = max(covered[0], end)

        interleave("vector", 0, 48)
        interleave("scalar", 48, 80)
        quantise_w(W_TILES - 2, 2)
        transpose_tiles(0)
        interleave("vector", 80, 128)
        transpose_tiles(1)
        quantise(0)
        interleave("vector", 128, V_FIRST)
        interleave("scalar", V_FIRST, CHUNKS[0])
        covered[0] = CHUNKS[0]

        for step in range(len(groups)):
            ahead = step + 1 < len(groups)

            def nothing():
                pass

            def quantise_next():
                if ahead:
                    quantise(step + 1)

            if ahead and step > 0:
                transpose_tiles(step + 1)
            slots = [nothing] * (2 * GROUP_MAX)
            slots[Q_SLOT] = quantise_next
            multiply(step, slots)
            interleave_through(step + LEAD + 1, SHARES)
